import numpy as np
import ml_dtypes


def mxq(x, axis, fmt="e4m3"):
    dtype, down = {"e4m3": (ml_dtypes.float8_e4m3fn, 7), "e5m2": (ml_dtypes.float8_e5m2, 14)}[fmt]
    v = np.moveaxis(np.asarray(x, np.float32).astype(ml_dtypes.bfloat16).astype(np.float64), axis, -1)
    blocks = v.reshape(v.shape[:-1] + (-1, 32))
    amax = np.abs(blocks).max(-1, keepdims=True)
    byte = np.maximum(np.where(amax > 0, np.frexp(amax)[1] - 1 + 127, 0) - down, 1)
    scale = np.exp2(byte - 127.0)
    codes = (blocks / scale).astype(np.float32).astype(dtype).astype(np.float64)
    return np.moveaxis((codes * scale).reshape(v.shape), -1, axis)


WIDE = False


def mx_kscale(k):
    if not WIDE:
        return np.ones(k)
    levels = np.array([10, -10, 5, -5, 0])
    a = np.random.permutation(np.resize(levels, k // 512 * 4)).reshape(k // 512, 4)
    idx = np.arange(k)
    return np.exp2(a[idx // 512, idx % 128 // 32])


BF16 = ml_dtypes.bfloat16


def bf(x):
    return np.asarray(x, np.float32).astype(BF16)


def f64(x):
    return np.asarray(x).astype(np.float64)


E2M1 = np.array([0.0, 0.5, 1.0, 1.5, 2.0, 3.0, 4.0, 6.0, -0.0, -0.5, -1.0, -1.5, -2.0, -3.0, -4.0, -6.0])


def pack_weight(w, fmt):
    k, n = w.shape
    w = f64(bf(w)).reshape(k // 32, 32, n)
    amax = np.abs(w).max(1)
    if fmt == "e4m3":
        byte = np.frexp(amax)[1] - 1 + 127 - 7
    else:
        mant, ex = np.frexp(amax / 6.0)
        byte = np.where(mant > 0.5, ex, ex - 1) + 127
    byte = np.clip(np.where(amax > 0, byte, 1), 1, 254)
    scaled = (w * np.exp2(127.0 - byte)[:, None, :]).reshape(k, n).astype(np.float32)
    by_word = np.ascontiguousarray(scaled.reshape(k // 512, 128, 4, n).transpose(0, 1, 3, 2))
    if fmt == "e4m3":
        words = by_word.astype(ml_dtypes.float8_e4m3fn).view(np.uint8)
    else:
        c = by_word.astype(ml_dtypes.float4_e2m1fn).view(np.uint8) & 0xF
        words = c[..., 0::2] | (c[..., 1::2] << 4)
    return np.ascontiguousarray(words), np.ascontiguousarray(byte.astype(np.uint8).reshape(k // 512, 16, n))


def unpack_weight(words, scales, fmt):
    g, p, n, _ = words.shape
    if fmt == "e4m3":
        vals = np.ascontiguousarray(words).view(ml_dtypes.float8_e4m3fn).astype(np.float64)
    else:
        nib = np.empty((g, p, n, 4), np.uint8)
        nib[..., 0::2] = words & 0xF
        nib[..., 1::2] = words >> 4
        vals = E2M1[nib]
    vals = vals * np.repeat(np.exp2(scales.astype(np.float64) - 127.0), 8, axis=1)[..., None]
    return vals.transpose(0, 1, 3, 2).reshape(g * 512, n)

def pack4(w):
    words, scales = pack_weight(w, "e2m1")
    return words.reshape(words.shape[0], 128, -1), scales


def unpack4(words, scales):
    return unpack_weight(words.reshape(words.shape[0], 128, -1, 2), scales, "e2m1")


B, K, N = 1024, 2048, 2048
EPS = 1e-5
GELU_C = 0.7978845608


def setup_inputs():
    s = mx_kscale(K)
    x = bf(np.random.standard_normal((B, K)) * s)
    words, scales = pack4(np.random.standard_normal((K, N)) * np.sqrt(2.0 / K) / s[:, None])
    return {"x": x,
            "weight_words": words,
            "weight_scales": scales,
            "bn_gamma": bf(np.random.uniform(0.5, 1.5, N)),
            "bn_beta": bf(np.random.standard_normal(N) * 0.1),
            "bn_mean": bf(np.random.standard_normal(N) * 0.1),
            "bn_var": bf(np.random.uniform(0.5, 1.5, N))}


def reference(x, weight_words, weight_scales, bn_gamma, bn_beta, bn_mean, bn_var):
    acc = mxq(f64(x), 1, "e4m3") @ unpack4(weight_words, weight_scales)
    x_norm = (acc - f64(bn_mean)) / np.sqrt(f64(bn_var) + EPS)
    bn_out = f64(bn_gamma) * x_norm + f64(bn_beta)
    gelu = 0.5 * bn_out * (1.0 + np.tanh(GELU_C * (bn_out + 0.044715 * bn_out * bn_out * bn_out)))
    return np.maximum(gelu, 0.0)

@@ -1,0 +1,220 @@
+from contextlib import ExitStack
+
+import concourse.mybir as mybir
+from concourse.masks import make_identity
+
+FLOPS = 2 * 1024 * 2048 * 2048
+
+BF16 = mybir.dt.bfloat16
+F32 = mybir.dt.float32
+I32 = mybir.dt.int32
+U8 = mybir.dt.uint8
+U32 = mybir.dt.uint32
+FP8X4 = mybir.dt.float8_e4m3fn_x4
+FP4X4 = mybir.dt.float4_e2m1fn_x4
+ACT = mybir.ActivationFunctionType
+ALU = mybir.AluOpType
+
+P = 128
+B, K, N = 1024, 2048, 2048
+G = K // 512
+MT = B // P
+NB = 512
+HALF = 1024
+EPS = 1e-5
+
+PIN = True
+ADD_ON_GPSIMD = (True, True, True, False)
+RELU_ON = ("s", "s", "s", "v")
+
+
+def tile_modelnew_kernel(tc, x, weight_words, weight_scales, bn_gamma, bn_beta, bn_mean, bn_var, out):
+    nc = tc.nc
+    with ExitStack() as ctx:
+        keep = ctx.enter_context(tc.tile_pool(name="keep", bufs=1))
+        grp_pool = ctx.enter_context(tc.tile_pool(name="grp", bufs=3))
+        y_pool = ctx.enter_context(tc.tile_pool(name="y", bufs=6))
+        ps_acc = ctx.enter_context(tc.psum_pool(name="ps_acc", bufs=5))
+        ps_xt = ctx.enter_context(tc.psum_pool(name="ps_xt", bufs=3))
+        if PIN:
+            ctx.enter_context(tc.manual_schedule())
+
+        w_sb = keep.tile([P, G, 2 * N], U8, name="w_sb", align_bytes=64)
+        w_sc = keep.tile([P, G, N], U8, name="w_sc", align_bytes=64)
+        x_sb = [keep.tile([P, K], BF16, name="x_sb%d" % m) for m in range(MT)]
+        xq = [keep.tile([P, G, P], U32, name="xq%d" % m, align_bytes=64) for m in range(MT)]
+        xs = [keep.tile([P, G, P], U8, name="xs%d" % m, align_bytes=64) for m in range(MT)]
+        ab_bc = keep.tile([P, 2, N], F32, name="ab_bc")
+        prm = keep.tile([P, P], BF16, name="prm")
+        ident_bf = keep.tile([P, P], BF16, name="ident_bf")
+        ident_f = keep.tile([P, P], F32, name="ident_f")
+        warm = keep.tile([P, 8], F32, name="warm")
+        vare = keep.tile([P, 16], F32, name="vare")
+        sd = keep.tile([P, 16], F32, name="sd")
+        rstd = keep.tile([P, 16], F32, name="rstd")
+        ma = keep.tile([P, 16], F32, name="ma")
+        ab_t = keep.tile([P, 2, 16], F32, name="ab_t")
+
+        for v, vec in enumerate((bn_gamma, bn_beta, bn_mean, bn_var)):
+            nc.scalar.dma_start(out=prm[16 * v:16 * v + 16, :], in_=vec.rearrange("(c j) -> c j", j=P))
+        nc.vector.memset(warm[:], 1.0)
+        nc.vector.memset(prm[64:128, :], 0.0)
+        nc.vector.memset(w_sc[:].bitcast(I32), 0)
+        make_identity(nc, ident_f[:])
+        make_identity(nc, ident_bf[:])
+        nc.scalar.activation(out=warm[:, 0:4], in_=warm[:, 4:8], func=ACT.Sqrt)
+
+        def load_x(m):
+            nc.sync.dma_start(out=x_sb[m][:], in_=x[P * m:P * (m + 1), :])
+
+        def load_w(h):
+            cols = slice(2 * HALF * h, 2 * HALF * (h + 1))
+            nc.sync.dma_start(
+                out=w_sb[:, :, cols].bitcast(I32),
+                in_=weight_words.rearrange("g p c -> p g c")[:, :, cols].bitcast(I32),
+            )
+
+        sc_rows = weight_scales.rearrange("g q n -> q g n")
+        nc.sync.dma_start(out=x_sb[0][:, 0:K // 2], in_=x[0:P, 0:K // 2])
+        nc.sync.dma_start(out=x_sb[0][:, K // 2:K], in_=x[0:P, K // 2:K])
+        load_x(1)
+        load_x(2)
+        for g0 in (0, 2):
+            for b in range(2):
+                for r in range(4):
+                    nc.sync.dma_start(
+                        out=w_sc[32 * b + r:P:64, g0:g0 + 2, :].bitcast(I32),
+                        in_=sc_rows[4 * b + r:16:8, g0:g0 + 2, :].bitcast(I32),
+                    )
+        load_w(0)
+        load_w(1)
+        for m in range(3, MT):
+            load_x(m)
+
+        grp_of = {}
+
+        def transposes(m, copy_engines):
+            xw = x_sb[m][:].bitcast(F32)
+            grp = grp_pool.tile([P, K], BF16, name="grp", align_bytes=64)
+            grp_of[m] = grp
+            gw = grp[:].bitcast(F32).rearrange("p (g b u) -> p g b u", g=G, b=P, u=2)
+            banks = []
+            for gp in range(2):
+                xt = ps_xt.tile([P, 2, 2, P], F32, name="xt", tag="xt")
+                for gg in range(2):
+                    g = 2 * gp + gg
+                    for u in range(2):
+                        nc.tensor.transpose(xt[:, gg, u, :], xw[:, 256 * g + u:256 * (g + 1):2], ident_f[:])
+                banks.append(xt)
+            for gp in range(2):
+                src = banks[gp][:].rearrange("p g u b -> p g b u")
+                dst = gw[:, 2 * gp:2 * gp + 2, :, :]
+                if copy_engines[gp] == "v":
+                    nc.vector.tensor_copy(out=dst, in_=src)
+                else:
+                    nc.scalar.copy(out=dst, in_=src)
+
+        def quantise(m):
+            nc.vector.quantize_mx(
+                out=xq[m][:].rearrange("p g b -> p (g b)").bitcast(FP8X4),
+                scales=xs[m][:].rearrange("p g b -> p (g b)"),
+                in_=grp_of[m][:],
+            )
+
+        def passes(m, i):
+            acc = ps_acc.tile([P, NB], F32, name="acc", tag="acc")
+            for g in range(G):
+                nc.tensor.matmul_mx(
+                    out=acc[:],
+                    lhsT=xq[m][:, g, :].bitcast(FP8X4),
+                    lhsT_scale=xs[m][:, g, :],
+                    rhs=w_sb[:, g, 2 * NB * i:2 * NB * (i + 1)].bitcast(FP4X4),
+                    rhs_scale=w_sc[:, g, NB * i:NB * (i + 1)],
+                    start=(g == 0),
+                    stop=(g == G - 1),
+                )
+            return acc
+
+        prm_t = ps_xt.tile([P, P], BF16, name="prm_t", tag="xt")
+        nc.tensor.transpose(prm_t[:], prm[:], ident_bf[:])
+        nc.vector.tensor_scalar_add(out=vare[:], in0=prm_t[:, 48:64], scalar1=EPS)
+        nc.scalar.activation(out=sd[:], in_=vare[:], func=ACT.Sqrt)
+        nc.vector.reciprocal(out=rstd[:], in_=sd[:])
+        nc.vector.tensor_mul(out=ab_t[:, 0, :], in0=prm_t[:, 0:16], in1=rstd[:])
+        nc.vector.tensor_mul(out=ma[:], in0=prm_t[:, 32:48], in1=ab_t[:, 0, :])
+        nc.vector.tensor_sub(out=ab_t[:, 1, :], in0=prm_t[:, 16:32], in1=ma[:])
+
+        transposes(0, "sv")
+        transposes(1, "sv")
+        quantise(0)
+        transposes(2, "sv")
+        nc.scalar.activation(out=warm[:, 0:4], in_=warm[:, 4:8], func=ACT.Gelu_apprx_tanh)
+        quantise(1)
+
+        for i in range(N // NB):
+            for v in range(2):
+                bc = ps_acc.tile([P, NB], F32, name="bc", tag="acc")
+                for cc in range(4):
+                    c = 4 * i + cc
+                    nc.tensor.transpose(
+                        bc[:, P * cc:P * (cc + 1)], ab_t[:, v, c:c + 1].to_broadcast([P, P]), ident_f[:]
+                    )
+                dst = ab_bc[:, v, NB * i:NB * (i + 1)]
+                if v == 0:
+                    nc.vector.tensor_copy(out=dst, in_=bc[:])
+                else:
+                    nc.scalar.copy(out=dst, in_=bc[:])
+        quantise(2)
+
+        units = [(0, 0), (1, 0), (2, 0), (0, 1), (1, 1), (2, 1)]
+        for m in range(3, MT):
+            units.extend([(m, 0), (m, 1)])
+        ahead = {3: 3, 6: 4, 8: 5, 10: 6, 12: 7}
+
+        def finish(unit, y, last):
+            m, h = unit
+            for j in range(2):
+                i = 2 * h + j
+                cols = slice(NB * j, NB * (j + 1))
+                who = "v" if last else RELU_ON[i]
+                if who == "v":
+                    nc.vector.tensor_scalar_max(out=y[:, cols], in0=y[:, cols], scalar1=0.0)
+                elif who == "g":
+                    nc.gpsimd.tensor_scalar(out=y[:, cols], in0=y[:, cols], scalar1=0.0, scalar2=0.0,
+                                            op0=ALU.max, op1=ALU.add)
+                if last:
+                    nc.sync.dma_start(out=out[P * m:P * (m + 1), NB * i:NB * (i + 1)], in_=y[:, cols])
+            if not last:
+                nc.sync.dma_start(out=out[P * m:P * (m + 1), HALF * h:HALF * (h + 1)], in_=y[:])
+
+        waiting = None
+        for k, (m, h) in enumerate(units):
+            last = k == len(units) - 1
+            nxt = ahead.get(k)
+            if nxt is not None:
+                transposes(nxt, "vv")
+            y = y_pool.tile([P, HALF], F32, name="y")
+            for j in range(2):
+                i = 2 * h + j
+                acc = passes(m, i)
+                nc.vector.tensor_mul(out=y[:, NB * j:NB * (j + 1)], in0=acc[:], in1=ab_bc[:, 0, NB * i:NB * (i + 1)])
+                if j == 0 and nxt is not None:
+                    quantise(nxt)
+            for j in range(2):
+                i = 2 * h + j
+                cols = slice(NB * j, NB * (j + 1))
+                shift = ab_bc[:, 1, NB * i:NB * (i + 1)]
+                if ADD_ON_GPSIMD[i] and not last:
+                    nc.gpsimd.tensor_add(out=y[:, cols], in0=y[:, cols], in1=shift)
+                else:
+                    nc.vector.tensor_add(out=y[:, cols], in0=y[:, cols], in1=shift)
+            for j in range(2):
+                i = 2 * h + j
+                cols = slice(NB * j, NB * (j + 1))
+                nc.scalar.activation(out=y[:, cols], in_=y[:, cols], func=ACT.Gelu_apprx_tanh)
+                if RELU_ON[i] == "s" and not last:
+                    nc.scalar.activation(out=y[:, cols], in_=y[:, cols], func=ACT.Relu)
+            if waiting is not None:
+                finish(waiting[0], waiting[1], False)
+            waiting = ((m, h), y)
+        finish(waiting[0], waiting[1], True)

@@ -24,8 +24,6 @@ HALF = 1024
 EPS = 1e-5
 
 PIN = True
-ADD_ON_GPSIMD = (True, True, True, False)
-RELU_ON = ("s", "s", "s", "v")
 
 
 def tile_modelnew_kernel(tc, x, weight_words, weight_scales, bn_gamma, bn_beta, bn_mean, bn_var, out):
@@ -171,23 +169,6 @@ def tile_modelnew_kernel(tc, x, weight_words, weight_scales, bn_gamma, bn_beta, 
             units.extend([(m, 0), (m, 1)])
         ahead = {3: 3, 6: 4, 8: 5, 10: 6, 12: 7}
 
-        def finish(unit, y, last):
-            m, h = unit
-            for j in range(2):
-                i = 2 * h + j
-                cols = slice(NB * j, NB * (j + 1))
-                who = "v" if last else RELU_ON[i]
-                if who == "v":
-                    nc.vector.tensor_scalar_max(out=y[:, cols], in0=y[:, cols], scalar1=0.0)
-                elif who == "g":
-                    nc.gpsimd.tensor_scalar(out=y[:, cols], in0=y[:, cols], scalar1=0.0, scalar2=0.0,
-                                            op0=ALU.max, op1=ALU.add)
-                if last:
-                    nc.sync.dma_start(out=out[P * m:P * (m + 1), NB * i:NB * (i + 1)], in_=y[:, cols])
-            if not last:
-                nc.sync.dma_start(out=out[P * m:P * (m + 1), HALF * h:HALF * (h + 1)], in_=y[:])
-
-        waiting = None
         for k, (m, h) in enumerate(units):
             last = k == len(units) - 1
             nxt = ahead.get(k)
@@ -200,21 +181,20 @@ def tile_modelnew_kernel(tc, x, weight_words, weight_scales, bn_gamma, bn_beta, 
                 nc.vector.tensor_mul(out=y[:, NB * j:NB * (j + 1)], in0=acc[:], in1=ab_bc[:, 0, NB * i:NB * (i + 1)])
                 if j == 0 and nxt is not None:
                     quantise(nxt)
-            for j in range(2):
-                i = 2 * h + j
-                cols = slice(NB * j, NB * (j + 1))
-                shift = ab_bc[:, 1, NB * i:NB * (i + 1)]
-                if ADD_ON_GPSIMD[i] and not last:
-                    nc.gpsimd.tensor_add(out=y[:, cols], in0=y[:, cols], in1=shift)
-                else:
-                    nc.vector.tensor_add(out=y[:, cols], in0=y[:, cols], in1=shift)
-            for j in range(2):
-                i = 2 * h + j
-                cols = slice(NB * j, NB * (j + 1))
-                nc.scalar.activation(out=y[:, cols], in_=y[:, cols], func=ACT.Gelu_apprx_tanh)
-                if RELU_ON[i] == "s" and not last:
-                    nc.scalar.activation(out=y[:, cols], in_=y[:, cols], func=ACT.Relu)
-            if waiting is not None:
-                finish(waiting[0], waiting[1], False)
-            waiting = ((m, h), y)
-        finish(waiting[0], waiting[1], True)
+            rows = slice(P * m, P * (m + 1))
+            if not last:
+                nc.gpsimd.tensor_add(out=y[:], in0=y[:], in1=ab_bc[:, 1, HALF * h:HALF * (h + 1)])
+                nc.scalar.activation(out=y[:], in_=y[:], func=ACT.Gelu_apprx_tanh)
+                nc.scalar.activation(out=y[:], in_=y[:], func=ACT.Relu)
+                nc.sync.dma_start(out=out[rows, HALF * h:HALF * (h + 1)], in_=y[:])
+            else:
+                for j in range(2):
+                    i = 2 * h + j
+                    cols = slice(NB * j, NB * (j + 1))
+                    nc.vector.tensor_add(out=y[:, cols], in0=y[:, cols], in1=ab_bc[:, 1, NB * i:NB * (i + 1)])
+                for j in range(2):
+                    i = 2 * h + j
+                    cols = slice(NB * j, NB * (j + 1))
+                    nc.scalar.activation(out=y[:, cols], in_=y[:, cols], func=ACT.Gelu_apprx_tanh)
+                    nc.vector.tensor_scalar_max(out=y[:, cols], in0=y[:, cols], scalar1=0.0)
+                    nc.sync.dma_start(out=out[rows, NB * i:NB * (i + 1)], in_=y[:, cols])

@@ -13,7 +13,6 @@ U32 = mybir.dt.uint32
 FP8X4 = mybir.dt.float8_e4m3fn_x4
 FP4X4 = mybir.dt.float4_e2m1fn_x4
 ACT = mybir.ActivationFunctionType
-ALU = mybir.AluOpType
 
 P = 128
 B, K, N = 1024, 2048, 2048
@@ -23,8 +22,6 @@ NB = 512
 HALF = 1024
 EPS = 1e-5
 
-PIN = True
-
 
 def tile_modelnew_kernel(tc, x, weight_words, weight_scales, bn_gamma, bn_beta, bn_mean, bn_var, out):
     nc = tc.nc
@@ -33,16 +30,18 @@ def tile_modelnew_kernel(tc, x, weight_words, weight_scales, bn_gamma, bn_beta, 
         grp_pool = ctx.enter_context(tc.tile_pool(name="grp", bufs=3))
         y_pool = ctx.enter_context(tc.tile_pool(name="y", bufs=6))
         ps_acc = ctx.enter_context(tc.psum_pool(name="ps_acc", bufs=5))
-        ps_xt = ctx.enter_context(tc.psum_pool(name="ps_xt", bufs=3))
-        if PIN:
-            ctx.enter_context(tc.manual_schedule())
+        ps_xt = ctx.enter_context(tc.psum_pool(name="ps_xt", bufs=2))
+        ps_keep = ctx.enter_context(tc.psum_pool(name="ps_keep", bufs=1))
+        ctx.enter_context(tc.manual_schedule())
 
         w_sb = keep.tile([P, G, 2 * N], U8, name="w_sb", align_bytes=64)
         w_sc = keep.tile([P, G, N], U8, name="w_sc", align_bytes=64)
         x_sb = [keep.tile([P, K], BF16, name="x_sb%d" % m) for m in range(MT)]
         xq = [keep.tile([P, G, P], U32, name="xq%d" % m, align_bytes=64) for m in range(MT)]
         xs = [keep.tile([P, G, P], U8, name="xs%d" % m, align_bytes=64) for m in range(MT)]
-        ab_bc = keep.tile([P, 2, N], F32, name="ab_bc")
+        a_bc = keep.tile([P, N], F32, name="a_bc")
+        b_bc = keep.tile([P, 3 * NB], F32, name="b_bc")
+        b_ps = ps_keep.tile([P, NB], F32, name="b_ps")
         prm = keep.tile([P, P], BF16, name="prm")
         ident_bf = keep.tile([P, P], BF16, name="ident_bf")
         ident_f = keep.tile([P, P], F32, name="ident_f")
@@ -55,11 +54,13 @@ def tile_modelnew_kernel(tc, x, weight_words, weight_scales, bn_gamma, bn_beta, 
 
         for v, vec in enumerate((bn_gamma, bn_beta, bn_mean, bn_var)):
             nc.scalar.dma_start(out=prm[16 * v:16 * v + 16, :], in_=vec.rearrange("(c j) -> c j", j=P))
+        nc.vector.memset(ident_f[:], 0.0)
         nc.vector.memset(warm[:], 1.0)
+        nc.vector.memset(ident_bf[:], 0.0)
         nc.vector.memset(prm[64:128, :], 0.0)
         nc.vector.memset(w_sc[:].bitcast(I32), 0)
-        make_identity(nc, ident_f[:])
-        make_identity(nc, ident_bf[:])
+        make_identity(nc, ident_f[:], nomemset=True)
+        make_identity(nc, ident_bf[:], nomemset=True)
         nc.scalar.activation(out=warm[:, 0:4], in_=warm[:, 4:8], func=ACT.Sqrt)
 
         def load_x(m):
@@ -133,7 +134,12 @@ def tile_modelnew_kernel(tc, x, weight_words, weight_scales, bn_gamma, bn_beta, 
                 )
             return acc
 
-        prm_t = ps_xt.tile([P, P], BF16, name="prm_t", tag="xt")
+        def shift_of(i):
+            return b_ps[:] if i == 3 else b_bc[:, NB * i:NB * (i + 1)]
+
+        transposes(0, "sv")
+
+        prm_t = ps_acc.tile([P, P], BF16, name="prm_t", tag="acc")
         nc.tensor.transpose(prm_t[:], prm[:], ident_bf[:])
         nc.vector.tensor_scalar_add(out=vare[:], in0=prm_t[:, 48:64], scalar1=EPS)
         nc.scalar.activation(out=sd[:], in_=vare[:], func=ACT.Sqrt)
@@ -142,7 +148,6 @@ def tile_modelnew_kernel(tc, x, weight_words, weight_scales, bn_gamma, bn_beta, 
         nc.vector.tensor_mul(out=ma[:], in0=prm_t[:, 32:48], in1=ab_t[:, 0, :])
         nc.vector.tensor_sub(out=ab_t[:, 1, :], in0=prm_t[:, 16:32], in1=ma[:])
 
-        transposes(0, "sv")
         transposes(1, "sv")
         quantise(0)
         transposes(2, "sv")
@@ -151,50 +156,61 @@ def tile_modelnew_kernel(tc, x, weight_words, weight_scales, bn_gamma, bn_beta, 
 
         for i in range(N // NB):
             for v in range(2):
-                bc = ps_acc.tile([P, NB], F32, name="bc", tag="acc")
+                if v == 1 and i == 3:
+                    bc = b_ps
+                else:
+                    bc = ps_acc.tile([P, NB], F32, name="bc", tag="acc")
                 for cc in range(4):
                     c = 4 * i + cc
                     nc.tensor.transpose(
                         bc[:, P * cc:P * (cc + 1)], ab_t[:, v, c:c + 1].to_broadcast([P, P]), ident_f[:]
                     )
-                dst = ab_bc[:, v, NB * i:NB * (i + 1)]
                 if v == 0:
-                    nc.vector.tensor_copy(out=dst, in_=bc[:])
-                else:
-                    nc.scalar.copy(out=dst, in_=bc[:])
+                    nc.vector.tensor_copy(out=a_bc[:, NB * i:NB * (i + 1)], in_=bc[:])
+                elif i < 3:
+                    nc.scalar.copy(out=b_bc[:, NB * i:NB * (i + 1)], in_=bc[:])
         quantise(2)
 
         units = [(0, 0), (1, 0), (2, 0), (0, 1), (1, 1), (2, 1)]
         for m in range(3, MT):
             units.extend([(m, 0), (m, 1)])
         ahead = {3: 3, 6: 4, 8: 5, 10: 6, 12: 7}
+        n_units = len(units)
 
+        def relu_store(bank, on_vector):
+            k, m, i, y = bank
+            j = i % 2
+            cols = slice(NB * j, NB * (j + 1))
+            rows = slice(P * m, P * (m + 1))
+            if on_vector:
+                nc.vector.tensor_scalar_max(out=y[:, cols], in0=y[:, cols], scalar1=0.0)
+            else:
+                nc.scalar.activation(out=y[:, cols], in_=y[:, cols], func=ACT.Relu)
+            if k >= n_units - 2:
+                nc.sync.dma_start(out=out[rows, NB * i:NB * (i + 1)], in_=y[:, cols])
+            elif j == 1:
+                nc.sync.dma_start(out=out[rows, NB * (i - 1):NB * (i + 1)], in_=y[:])
+
+        before = None
         for k, (m, h) in enumerate(units):
-            last = k == len(units) - 1
+            tail = k >= n_units - 2
             nxt = ahead.get(k)
             if nxt is not None:
                 transposes(nxt, "vv")
             y = y_pool.tile([P, HALF], F32, name="y")
             for j in range(2):
                 i = 2 * h + j
+                cols = slice(NB * j, NB * (j + 1))
                 acc = passes(m, i)
-                nc.vector.tensor_mul(out=y[:, NB * j:NB * (j + 1)], in0=acc[:], in1=ab_bc[:, 0, NB * i:NB * (i + 1)])
+                nc.vector.tensor_mul(out=y[:, cols], in0=acc[:], in1=a_bc[:, NB * i:NB * (i + 1)])
+                if i == 3 or (tail and i == 1):
+                    nc.vector.tensor_add(out=y[:, cols], in0=y[:, cols], in1=shift_of(i))
+                else:
+                    nc.gpsimd.tensor_add(out=y[:, cols], in0=y[:, cols], in1=shift_of(i))
                 if j == 0 and nxt is not None:
                     quantise(nxt)
-            rows = slice(P * m, P * (m + 1))
-            if not last:
-                nc.gpsimd.tensor_add(out=y[:], in0=y[:], in1=ab_bc[:, 1, HALF * h:HALF * (h + 1)])
-                nc.scalar.activation(out=y[:], in_=y[:], func=ACT.Gelu_apprx_tanh)
-                nc.scalar.activation(out=y[:], in_=y[:], func=ACT.Relu)
-                nc.sync.dma_start(out=out[rows, HALF * h:HALF * (h + 1)], in_=y[:])
-            else:
-                for j in range(2):
-                    i = 2 * h + j
-                    cols = slice(NB * j, NB * (j + 1))
-                    nc.vector.tensor_add(out=y[:, cols], in0=y[:, cols], in1=ab_bc[:, 1, NB * i:NB * (i + 1)])
-                for j in range(2):
-                    i = 2 * h + j
-                    cols = slice(NB * j, NB * (j + 1))
-                    nc.scalar.activation(out=y[:, cols], in_=y[:, cols], func=ACT.Gelu_apprx_tanh)
-                    nc.vector.tensor_scalar_max(out=y[:, cols], in0=y[:, cols], scalar1=0.0)
-                    nc.sync.dma_start(out=out[rows, NB * i:NB * (i + 1)], in_=y[:, cols])
+                nc.scalar.activation(out=y[:, cols], in_=y[:, cols], func=ACT.Gelu_apprx_tanh)
+                if before is not None:
+                    relu_store(before, False)
+                before = (k, m, i, y)
+        relu_store(before, True)

@@ -78,13 +78,11 @@ def tile_modelnew_kernel(tc, x, weight_words, weight_scales, bn_gamma, bn_beta, 
         nc.sync.dma_start(out=x_sb[0][:, K // 2:K], in_=x[0:P, K // 2:K])
         load_x(1)
         load_x(2)
-        for g0 in (0, 2):
-            for b in range(2):
-                for r in range(4):
-                    nc.sync.dma_start(
-                        out=w_sc[32 * b + r:P:64, g0:g0 + 2, :].bitcast(I32),
-                        in_=sc_rows[4 * b + r:16:8, g0:g0 + 2, :].bitcast(I32),
-                    )
+        for b in range(2):
+            for r in range(4):
+                nc.sync.dma_start(
+                    out=w_sc[32 * b + r:P:64, :, :].bitcast(I32), in_=sc_rows[4 * b + r:16:8, :, :].bitcast(I32)
+                )
         load_w(0)
         load_w(1)
         for m in range(3, MT):
@@ -192,6 +190,7 @@ def tile_modelnew_kernel(tc, x, weight_words, weight_scales, bn_gamma, bn_beta, 
                 nc.sync.dma_start(out=out[rows, NB * (i - 1):NB * (i + 1)], in_=y[:])
 
         before = None
+        at_end = []
         for k, (m, h) in enumerate(units):
             tail = k >= n_units - 2
             nxt = ahead.get(k)
@@ -212,5 +211,10 @@ def tile_modelnew_kernel(tc, x, weight_words, weight_scales, bn_gamma, bn_beta, 
                 nc.scalar.activation(out=y[:, cols], in_=y[:, cols], func=ACT.Gelu_apprx_tanh)
                 if before is not None:
                     relu_store(before, False)
-                before = (k, m, i, y)
-        relu_store(before, True)
+                    before = None
+                if m == MT - 1 and i >= 1:
+                    at_end.append((k, m, i, y))
+                else:
+                    before = (k, m, i, y)
+        for bank in at_end:
+            relu_store(bank, True)

@@ -184,7 +184,7 @@ def tile_modelnew_kernel(tc, x, weight_words, weight_scales, bn_gamma, bn_beta, 
                 nc.vector.tensor_scalar_max(out=y[:, cols], in0=y[:, cols], scalar1=0.0)
             else:
                 nc.scalar.activation(out=y[:, cols], in_=y[:, cols], func=ACT.Relu)
-            if k >= n_units - 2:
+            if k >= n_units - 4:
                 nc.sync.dma_start(out=out[rows, NB * i:NB * (i + 1)], in_=y[:, cols])
             elif j == 1:
                 nc.sync.dma_start(out=out[rows, NB * (i - 1):NB * (i + 1)], in_=y[:])
@@ -212,7 +212,7 @@ def tile_modelnew_kernel(tc, x, weight_words, weight_scales, bn_gamma, bn_beta, 
                 if before is not None:
                     relu_store(before, False)
                     before = None
-                if m == MT - 1 and i >= 1:
+                if m == MT - 1:
                     at_end.append((k, m, i, y))
                 else:
                     before = (k, m, i, y)

@@ -46,6 +46,7 @@ def tile_modelnew_kernel(tc, x, weight_words, weight_scales, bn_gamma, bn_beta, 
         ident_bf = keep.tile([P, P], BF16, name="ident_bf")
         ident_f = keep.tile([P, P], F32, name="ident_f")
         warm = keep.tile([P, 8], F32, name="warm")
+        idle_in = keep.tile([P, NB], BF16, name="idle_in")
         vare = keep.tile([P, 16], F32, name="vare")
         sd = keep.tile([P, 16], F32, name="sd")
         rstd = keep.tile([P, 16], F32, name="rstd")
@@ -54,6 +55,7 @@ def tile_modelnew_kernel(tc, x, weight_words, weight_scales, bn_gamma, bn_beta, 
 
         for v, vec in enumerate((bn_gamma, bn_beta, bn_mean, bn_var)):
             nc.scalar.dma_start(out=prm[16 * v:16 * v + 16, :], in_=vec.rearrange("(c j) -> c j", j=P))
+        nc.gpsimd.memset(idle_in[:], 0.0)
         nc.vector.memset(ident_f[:], 0.0)
         nc.vector.memset(warm[:], 1.0)
         nc.vector.memset(ident_bf[:], 0.0)
@@ -90,7 +92,10 @@ def tile_modelnew_kernel(tc, x, weight_words, weight_scales, bn_gamma, bn_beta, 
 
         grp_of = {}
 
-        def transposes(m, copy_engines):
+        def clock_keeper(width):
+            nc.tensor.matmul(b_ps[:, 0:width], lhsT=idle_in[:, 0:P], rhs=idle_in[:, 0:width], start=True, stop=True)
+
+        def transposes(m, copy_engines, keep_clock=False):
             xw = x_sb[m][:].bitcast(F32)
             grp = grp_pool.tile([P, K], BF16, name="grp", align_bytes=64)
             grp_of[m] = grp
@@ -102,6 +107,8 @@ def tile_modelnew_kernel(tc, x, weight_words, weight_scales, bn_gamma, bn_beta, 
                     g = 2 * gp + gg
                     for u in range(2):
                         nc.tensor.transpose(xt[:, gg, u, :], xw[:, 256 * g + u:256 * (g + 1):2], ident_f[:])
+                if keep_clock:
+                    clock_keeper(NB)
                 banks.append(xt)
             for gp in range(2):
                 src = banks[gp][:].rearrange("p g u b -> p g b u")
@@ -135,7 +142,9 @@ def tile_modelnew_kernel(tc, x, weight_words, weight_scales, bn_gamma, bn_beta, 
         def shift_of(i):
             return b_ps[:] if i == 3 else b_bc[:, NB * i:NB * (i + 1)]
 
-        transposes(0, "sv")
+        for d in range(6):
+            clock_keeper(NB)
+        transposes(0, "sv", True)
 
         prm_t = ps_acc.tile([P, P], BF16, name="prm_t", tag="acc")
         nc.tensor.transpose(prm_t[:], prm[:], ident_bf[:])
@@ -146,9 +155,9 @@ def tile_modelnew_kernel(tc, x, weight_words, weight_scales, bn_gamma, bn_beta, 
         nc.vector.tensor_mul(out=ma[:], in0=prm_t[:, 32:48], in1=ab_t[:, 0, :])
         nc.vector.tensor_sub(out=ab_t[:, 1, :], in0=prm_t[:, 16:32], in1=ma[:])
 
-        transposes(1, "sv")
+        transposes(1, "sv", True)
         quantise(0)
-        transposes(2, "sv")
+        transposes(2, "sv", True)
         nc.scalar.activation(out=warm[:, 0:4], in_=warm[:, 4:8], func=ACT.Gelu_apprx_tanh)
         quantise(1)
 
@@ -163,6 +172,8 @@ def tile_modelnew_kernel(tc, x, weight_words, weight_scales, bn_gamma, bn_beta, 
                     nc.tensor.transpose(
                         bc[:, P * cc:P * (cc + 1)], ab_t[:, v, c:c + 1].to_broadcast([P, P]), ident_f[:]
                     )
+                if bc is not b_ps:
+                    clock_keeper(NB // 2)
                 if v == 0:
                     nc.vector.tensor_copy(out=a_bc[:, NB * i:NB * (i + 1)], in_=bc[:])
                 elif i < 3:

@@ -108,7 +108,7 @@ def tile_modelnew_kernel(tc, x, weight_words, weight_scales, bn_gamma, bn_beta, 
                     for u in range(2):
                         nc.tensor.transpose(xt[:, gg, u, :], xw[:, 256 * g + u:256 * (g + 1):2], ident_f[:])
                 if keep_clock:
-                    clock_keeper(NB)
+                    clock_keeper(NB // 2)
                 banks.append(xt)
             for gp in range(2):
                 src = banks[gp][:].rearrange("p g u b -> p g b u")
@@ -172,7 +172,7 @@ def tile_modelnew_kernel(tc, x, weight_words, weight_scales, bn_gamma, bn_beta, 
                     nc.tensor.transpose(
                         bc[:, P * cc:P * (cc + 1)], ab_t[:, v, c:c + 1].to_broadcast([P, P]), ident_f[:]
                     )
-                if bc is not b_ps:
+                if v == 0:
                     clock_keeper(NB // 2)
                 if v == 0:
                     nc.vector.tensor_copy(out=a_bc[:, NB * i:NB * (i + 1)], in_=bc[:])

@@ -28,7 +28,7 @@ def tile_modelnew_kernel(tc, x, weight_words, weight_scales, bn_gamma, bn_beta, 
     with ExitStack() as ctx:
         keep = ctx.enter_context(tc.tile_pool(name="keep", bufs=1))
         grp_pool = ctx.enter_context(tc.tile_pool(name="grp", bufs=3))
-        y_pool = ctx.enter_context(tc.tile_pool(name="y", bufs=6))
+        y_pool = ctx.enter_context(tc.tile_pool(name="y", bufs=10))
         ps_acc = ctx.enter_context(tc.psum_pool(name="ps_acc", bufs=5))
         ps_xt = ctx.enter_context(tc.psum_pool(name="ps_xt", bufs=2))
         ps_keep = ctx.enter_context(tc.psum_pool(name="ps_keep", bufs=1))

@@ -47,7 +47,6 @@ def tile_modelnew_kernel(tc, x, weight_words, weight_scales, bn_gamma, bn_beta, 
         ident_f = keep.tile([P, P], F32, name="ident_f")
         warm = keep.tile([P, 8], F32, name="warm")
         idle_in = keep.tile([P, NB], BF16, name="idle_in")
-        vare = keep.tile([P, 16], F32, name="vare")
         sd = keep.tile([P, 16], F32, name="sd")
         rstd = keep.tile([P, 16], F32, name="rstd")
         ma = keep.tile([P, 16], F32, name="ma")
@@ -148,8 +147,7 @@ def tile_modelnew_kernel(tc, x, weight_words, weight_scales, bn_gamma, bn_beta, 
 
         prm_t = ps_acc.tile([P, P], BF16, name="prm_t", tag="acc")
         nc.tensor.transpose(prm_t[:], prm[:], ident_bf[:])
-        nc.vector.tensor_scalar_add(out=vare[:], in0=prm_t[:, 48:64], scalar1=EPS)
-        nc.scalar.activation(out=sd[:], in_=vare[:], func=ACT.Sqrt)
+        nc.scalar.activation(out=sd[:], in_=prm_t[:, 48:64], func=ACT.Sqrt, bias=EPS)
         nc.vector.reciprocal(out=rstd[:], in_=sd[:])
         nc.vector.tensor_mul(out=ab_t[:, 0, :], in0=prm_t[:, 0:16], in1=rstd[:])
         nc.vector.tensor_mul(out=ma[:], in0=prm_t[:, 32:48], in1=ab_t[:, 0, :])
@@ -158,7 +156,6 @@ def tile_modelnew_kernel(tc, x, weight_words, weight_scales, bn_gamma, bn_beta, 
         transposes(1, "sv", True)
         quantise(0)
         transposes(2, "sv", True)
-        nc.scalar.activation(out=warm[:, 0:4], in_=warm[:, 4:8], func=ACT.Gelu_apprx_tanh)
         quantise(1)
 
         for i in range(N // NB):
@@ -174,10 +171,13 @@ def tile_modelnew_kernel(tc, x, weight_words, weight_scales, bn_gamma, bn_beta, 
                     )
                 if v == 0:
                     clock_keeper(NB // 2)
-                if v == 0:
+                if v == 0 and i >= 2:
                     nc.vector.tensor_copy(out=a_bc[:, NB * i:NB * (i + 1)], in_=bc[:])
+                elif v == 0:
+                    nc.scalar.copy(out=a_bc[:, NB * i:NB * (i + 1)], in_=bc[:])
                 elif i < 3:
                     nc.scalar.copy(out=b_bc[:, NB * i:NB * (i + 1)], in_=bc[:])
+        nc.scalar.activation(out=warm[:, 0:4], in_=warm[:, 4:8], func=ACT.Gelu_apprx_tanh)
         quantise(2)
 
         units = [(0, 0), (1, 0), (2, 0), (0, 1), (1, 1), (2, 1)]

@@ -180,8 +180,8 @@ def tile_modelnew_kernel(tc, x, weight_words, weight_scales, bn_gamma, bn_beta, 
         nc.scalar.activation(out=warm[:, 0:4], in_=warm[:, 4:8], func=ACT.Gelu_apprx_tanh)
         quantise(2)
 
-        units = [(0, 0), (1, 0), (2, 0), (0, 1), (1, 1), (2, 1)]
-        for m in range(3, MT):
+        units = []
+        for m in range(MT):
             units.extend([(m, 0), (m, 1)])
         ahead = {3: 3, 6: 4, 8: 5, 10: 6, 12: 7}
         n_units = len(units)

from contextlib import ExitStack

import concourse.mybir as mybir
from concourse.masks import make_identity

FLOPS = 2 * 1024 * 2048 * 2048

BF16 = mybir.dt.bfloat16
F32 = mybir.dt.float32
I32 = mybir.dt.int32
U8 = mybir.dt.uint8
U32 = mybir.dt.uint32
FP8X4 = mybir.dt.float8_e4m3fn_x4
FP4X4 = mybir.dt.float4_e2m1fn_x4
ACT = mybir.ActivationFunctionType

P = 128
B, K, N = 1024, 2048, 2048
G = K // 512
MT = B // P
NB = 512
HALF = 1024
EPS = 1e-5


def tile_modelnew_kernel(tc, x, weight_words, weight_scales, bn_gamma, bn_beta, bn_mean, bn_var, out):
    nc = tc.nc
    with ExitStack() as ctx:
        keep = ctx.enter_context(tc.tile_pool(name="keep", bufs=1))
        grp_pool = ctx.enter_context(tc.tile_pool(name="grp", bufs=3))
        y_pool = ctx.enter_context(tc.tile_pool(name="y", bufs=10))
        ps_acc = ctx.enter_context(tc.psum_pool(name="ps_acc", bufs=5))
        ps_xt = ctx.enter_context(tc.psum_pool(name="ps_xt", bufs=2))
        ps_keep = ctx.enter_context(tc.psum_pool(name="ps_keep", bufs=1))
        ctx.enter_context(tc.manual_schedule())

        w_sb = keep.tile([P, G, 2 * N], U8, name="w_sb", align_bytes=64)
        w_sc = keep.tile([P, G, N], U8, name="w_sc", align_bytes=64)
        x_sb = [keep.tile([P, K], BF16, name="x_sb%d" % m) for m in range(MT)]
        xq = [keep.tile([P, G, P], U32, name="xq%d" % m, align_bytes=64) for m in range(MT)]
        xs = [keep.tile([P, G, P], U8, name="xs%d" % m, align_bytes=64) for m in range(MT)]
        a_bc = keep.tile([P, N], F32, name="a_bc")
        b_bc = keep.tile([P, 3 * NB], F32, name="b_bc")
        b_ps = ps_keep.tile([P, NB], F32, name="b_ps")
        prm = keep.tile([P, P], BF16, name="prm")
        ident_bf = keep.tile([P, P], BF16, name="ident_bf")
        ident_f = keep.tile([P, P], F32, name="ident_f")
        warm = keep.tile([P, 8], F32, name="warm")
        idle_in = keep.tile([P, NB], BF16, name="idle_in")
        sd = keep.tile([P, 16], F32, name="sd")
        rstd = keep.tile([P, 16], F32, name="rstd")
        ma = keep.tile([P, 16], F32, name="ma")
        ab_t = keep.tile([P, 2, 16], F32, name="ab_t")

        for v, vec in enumerate((bn_gamma, bn_beta, bn_mean, bn_var)):
            nc.scalar.dma_start(out=prm[16 * v:16 * v + 16, :], in_=vec.rearrange("(c j) -> c j", j=P))
        nc.gpsimd.memset(idle_in[:], 0.0)
        nc.vector.memset(ident_f[:], 0.0)
        nc.vector.memset(warm[:], 1.0)
        nc.vector.memset(ident_bf[:], 0.0)
        nc.vector.memset(prm[64:128, :], 0.0)
        nc.vector.memset(w_sc[:].bitcast(I32), 0)
        make_identity(nc, ident_f[:], nomemset=True)
        make_identity(nc, ident_bf[:], nomemset=True)
        nc.scalar.activation(out=warm[:, 0:4], in_=warm[:, 4:8], func=ACT.Sqrt)

        def load_x(m):
            nc.sync.dma_start(out=x_sb[m][:], in_=x[P * m:P * (m + 1), :])

        def load_w(h):
            cols = slice(2 * HALF * h, 2 * HALF * (h + 1))
            nc.sync.dma_start(
                out=w_sb[:, :, cols].bitcast(I32),
                in_=weight_words.rearrange("g p c -> p g c")[:, :, cols].bitcast(I32),
            )

        sc_rows = weight_scales.rearrange("g q n -> q g n")
        nc.sync.dma_start(out=x_sb[0][:, 0:K // 2], in_=x[0:P, 0:K // 2])
        nc.sync.dma_start(out=x_sb[0][:, K // 2:K], in_=x[0:P, K // 2:K])
        load_x(1)
        load_x(2)
        for b in range(2):
            for r in range(4):
                nc.sync.dma_start(
                    out=w_sc[32 * b + r:P:64, :, :].bitcast(I32), in_=sc_rows[4 * b + r:16:8, :, :].bitcast(I32)
                )
        load_w(0)
        load_w(1)
        for m in range(3, MT):
            load_x(m)

        grp_of = {}

        def clock_keeper(width):
            nc.tensor.matmul(b_ps[:, 0:width], lhsT=idle_in[:, 0:P], rhs=idle_in[:, 0:width], start=True, stop=True)

        def transposes(m, copy_engines, keep_clock=False):
            xw = x_sb[m][:].bitcast(F32)
            grp = grp_pool.tile([P, K], BF16, name="grp", align_bytes=64)
            grp_of[m] = grp
            gw = grp[:].bitcast(F32).rearrange("p (g b u) -> p g b u", g=G, b=P, u=2)
            banks = []
            for gp in range(2):
                xt = ps_xt.tile([P, 2, 2, P], F32, name="xt", tag="xt")
                for gg in range(2):
                    g = 2 * gp + gg
                    for u in range(2):
                        nc.tensor.transpose(xt[:, gg, u, :], xw[:, 256 * g + u:256 * (g + 1):2], ident_f[:])
                if keep_clock:
                    clock_keeper(NB // 2)
                banks.append(xt)
            for gp in range(2):
                src = banks[gp][:].rearrange("p g u b -> p g b u")
                dst = gw[:, 2 * gp:2 * gp + 2, :, :]
                if copy_engines[gp] == "v":
                    nc.vector.tensor_copy(out=dst, in_=src)
                else:
                    nc.scalar.copy(out=dst, in_=src)

        def quantise(m):
            nc.vector.quantize_mx(
                out=xq[m][:].rearrange("p g b -> p (g b)").bitcast(FP8X4),
                scales=xs[m][:].rearrange("p g b -> p (g b)"),
                in_=grp_of[m][:],
            )

        def passes(m, i):
            acc = ps_acc.tile([P, NB], F32, name="acc", tag="acc")
            for g in range(G):
                nc.tensor.matmul_mx(
                    out=acc[:],
                    lhsT=xq[m][:, g, :].bitcast(FP8X4),
                    lhsT_scale=xs[m][:, g, :],
                    rhs=w_sb[:, g, 2 * NB * i:2 * NB * (i + 1)].bitcast(FP4X4),
                    rhs_scale=w_sc[:, g, NB * i:NB * (i + 1)],
                    start=(g == 0),
                    stop=(g == G - 1),
                )
            return acc

        def shift_of(i):
            return b_ps[:] if i == 3 else b_bc[:, NB * i:NB * (i + 1)]

        for d in range(6):
            clock_keeper(NB)
        transposes(0, "sv", True)

        prm_t = ps_acc.tile([P, P], BF16, name="prm_t", tag="acc")
        nc.tensor.transpose(prm_t[:], prm[:], ident_bf[:])
        nc.scalar.activation(out=sd[:], in_=prm_t[:, 48:64], func=ACT.Sqrt, bias=EPS)
        nc.vector.reciprocal(out=rstd[:], in_=sd[:])
        nc.vector.tensor_mul(out=ab_t[:, 0, :], in0=prm_t[:, 0:16], in1=rstd[:])
        nc.vector.tensor_mul(out=ma[:], in0=prm_t[:, 32:48], in1=ab_t[:, 0, :])
        nc.vector.tensor_sub(out=ab_t[:, 1, :], in0=prm_t[:, 16:32], in1=ma[:])

        transposes(1, "sv", True)
        quantise(0)
        transposes(2, "sv", True)
        quantise(1)

        for i in range(N // NB):
            for v in range(2):
                if v == 1 and i == 3:
                    bc = b_ps
                else:
                    bc = ps_acc.tile([P, NB], F32, name="bc", tag="acc")
                for cc in range(4):
                    c = 4 * i + cc
                    nc.tensor.transpose(
                        bc[:, P * cc:P * (cc + 1)], ab_t[:, v, c:c + 1].to_broadcast([P, P]), ident_f[:]
                    )
                if v == 0:
                    clock_keeper(NB // 2)
                if v == 0 and i >= 2:
                    nc.vector.tensor_copy(out=a_bc[:, NB * i:NB * (i + 1)], in_=bc[:])
                elif v == 0:
                    nc.scalar.copy(out=a_bc[:, NB * i:NB * (i + 1)], in_=bc[:])
                elif i < 3:
                    nc.scalar.copy(out=b_bc[:, NB * i:NB * (i + 1)], in_=bc[:])
        nc.scalar.activation(out=warm[:, 0:4], in_=warm[:, 4:8], func=ACT.Gelu_apprx_tanh)
        quantise(2)

        units = []
        for m in range(MT):
            units.extend([(m, 0), (m, 1)])
        ahead = {3: 3, 6: 4, 8: 5, 10: 6, 12: 7}
        n_units = len(units)

        def relu_store(bank, on_vector):
            k, m, i, y = bank
            j = i % 2
            cols = slice(NB * j, NB * (j + 1))
            rows = slice(P * m, P * (m + 1))
            if on_vector:
                nc.vector.tensor_scalar_max(out=y[:, cols], in0=y[:, cols], scalar1=0.0)
            else:
                nc.scalar.activation(out=y[:, cols], in_=y[:, cols], func=ACT.Relu)
            if k >= n_units - 4:
                nc.sync.dma_start(out=out[rows, NB * i:NB * (i + 1)], in_=y[:, cols])
            elif j == 1:
                nc.sync.dma_start(out=out[rows, NB * (i - 1):NB * (i + 1)], in_=y[:])

        before = None
        at_end = []
        for k, (m, h) in enumerate(units):
            tail = k >= n_units - 2
            nxt = ahead.get(k)
            if nxt is not None:
                transposes(nxt, "vv")
            y = y_pool.tile([P, HALF], F32, name="y")
            for j in range(2):
                i = 2 * h + j
                cols = slice(NB * j, NB * (j + 1))
                acc = passes(m, i)
                nc.vector.tensor_mul(out=y[:, cols], in0=acc[:], in1=a_bc[:, NB * i:NB * (i + 1)])
                if i == 3 or (tail and i == 1):
                    nc.vector.tensor_add(out=y[:, cols], in0=y[:, cols], in1=shift_of(i))
                else:
                    nc.gpsimd.tensor_add(out=y[:, cols], in0=y[:, cols], in1=shift_of(i))
                if j == 0 and nxt is not None:
                    quantise(nxt)
                nc.scalar.activation(out=y[:, cols], in_=y[:, cols], func=ACT.Gelu_apprx_tanh)
                if before is not None:
                    relu_store(before, False)
                    before = None
                if m == MT - 1:
                    at_end.append((k, m, i, y))
                else:
                    before = (k, m, i, y)
        for bank in at_end:
            relu_store(bank, True)
